import numpy as np
import ml_dtypes

BF16 = ml_dtypes.bfloat16


def bf(x):
    return np.asarray(x, np.float32).astype(BF16)


def f32(x):
    return np.asarray(x, np.float32)


def f64(x):
    return np.asarray(x).astype(np.float64)


def striped(idx):
    return np.tile(idx.reshape(-1, 16).T, (8, 1))


H, E, M, S, N = 128, 128, 512, 512, 128


def sigmoid(v):
    return 1.0 / (1.0 + np.exp(-v))


def setup_inputs():
    return {
        "table": bf(np.random.standard_normal((H, S))),
        "w": bf(np.random.standard_normal((H, M)) / np.sqrt(H)),
        "x": bf(np.random.standard_normal((E, N))),
        "wx": bf(np.random.standard_normal((E, M)) / np.sqrt(E)),
        "b": f32(0.1 * np.random.standard_normal((M, 1))),
        "c": f32(np.random.standard_normal((H, N))),
        "offs": striped(np.random.permutation(S)[:N]),
    }


def reference(table, w, x, wx, b, c, offs):
    idx = offs[:16].T.reshape(-1)
    pre = f64(w).T @ f64(table)[:, idx] + f64(wx).T @ f64(x) + f64(b)
    p_in, p_out, p_upd, p_forget = np.split(pre, M // H)
    c_new = sigmoid(p_in) * np.tanh(p_upd) + sigmoid(p_forget) * f64(c)
    return sigmoid(p_out) * np.tanh(c_new)

@@ -1,0 +1,66 @@
+import concourse.mybir as mybir
+
+BF16, F32, U16 = mybir.dt.bfloat16, mybir.dt.float32, mybir.dt.uint16
+SIGMOID = mybir.ActivationFunctionType.Sigmoid
+TANH = mybir.ActivationFunctionType.Tanh
+
+P = 128
+S = 512
+N = 128
+GATES = 4
+IN_GATE, OUT_GATE, UPDATE, FORGET = 0, 1, 2, 3
+
+FLOPS = 2 * (P + P) * (GATES * P) * N
+
+
+def tile_narytreelstmcell_kernel(tc, table, w, x, wx, b, c, offs, out):
+    nc = tc.nc
+    with (
+        tc.tile_pool(name="held", bufs=1) as held,
+        tc.psum_pool(name="psum", bufs=1) as psum,
+    ):
+        offsets = held.tile([P, N // 16], U16, name="offsets")
+        nc.sync.dma_start(offsets[:], offs)
+        store = held.tile([P, S], BF16, name="store")
+        nc.sync.dma_start(store[:], table)
+        w_sb = held.tile([P, GATES * P], BF16, name="w_sb")
+        nc.scalar.dma_start(w_sb[:], w)
+        wx_sb = held.tile([P, GATES * P], BF16, name="wx_sb")
+        nc.scalar.dma_start(wx_sb[:], wx)
+        x_sb = held.tile([P, N], BF16, name="x_sb")
+        nc.sync.dma_start(x_sb[:], x)
+        c_sb = held.tile([P, N], F32, name="c_sb")
+        nc.gpsimd.dma_start(c_sb[:], c)
+        bias = held.tile([P, GATES], F32, name="bias")
+        with nc.allow_non_contiguous_dma(reason="512 bias values, one to a partition and gate"):
+            nc.sync.dma_start(bias[:], b.rearrange("(g r) o -> r (g o)", r=P))
+
+        pre = [psum.tile([P, N], F32, name=f"pre{g}") for g in range(GATES)]
+        gate_order = (FORGET, IN_GATE, UPDATE, OUT_GATE)
+        for g in gate_order:
+            nc.tensor.matmul(pre[g][:], wx_sb[:, g * P : (g + 1) * P], x_sb[:], start=True, stop=False)
+        for g in gate_order:
+            nc.tensor.matmul(
+                pre[g][:], w_sb[:, g * P : (g + 1) * P], store[:].indirect(offsets[:]), start=False, stop=True
+            )
+
+        def gate(g, func, name):
+            result = held.tile([P, N], F32, name=name)
+            nc.scalar.activation(result[:], pre[g][:], func, bias=bias[:, g : g + 1])
+            return result
+
+        forget = gate(FORGET, SIGMOID, "forget")
+        in_gate = gate(IN_GATE, SIGMOID, "in_gate")
+        update = gate(UPDATE, TANH, "update")
+        out_gate = gate(OUT_GATE, SIGMOID, "out_gate")
+
+        kept = held.tile([P, N], F32, name="kept")
+        nc.vector.tensor_mul(kept[:], forget[:], c_sb[:])
+        c_new = held.tile([P, N], F32, name="c_new")
+        nc.vector.tensor_mul(c_new[:], in_gate[:], update[:])
+        nc.vector.tensor_add(c_new[:], c_new[:], kept[:])
+        squashed = held.tile([P, N], F32, name="squashed")
+        nc.scalar.activation(squashed[:], c_new[:], TANH)
+        hidden = held.tile([P, N], F32, name="hidden")
+        nc.vector.tensor_mul(hidden[:], out_gate[:], squashed[:])
+        nc.sync.dma_start(out, hidden[:])

@@ -35,6 +35,10 @@ def tile_narytreelstmcell_kernel(tc, table, w, x, wx, b, c, offs, out):
         with nc.allow_non_contiguous_dma(reason="512 bias values, one to a partition and gate"):
             nc.sync.dma_start(bias[:], b.rearrange("(g r) o -> r (g o)", r=P))
 
+        scratch = held.tile([P, 1], F32, name="scratch")
+        nc.vector.memset(scratch[:], 0.0)
+        nc.scalar.activation(scratch[:], scratch[:], SIGMOID)
+
         pre = [psum.tile([P, N], F32, name=f"pre{g}") for g in range(GATES)]
         gate_order = (FORGET, IN_GATE, UPDATE, OUT_GATE)
         for g in gate_order:

@@ -10,6 +10,8 @@ N = 128
 GATES = 4
 IN_GATE, OUT_GATE, UPDATE, FORGET = 0, 1, 2, 3
 
+WARMING_MATMULS = 16
+
 FLOPS = 2 * (P + P) * (GATES * P) * N
 
 
@@ -39,14 +41,20 @@ def tile_narytreelstmcell_kernel(tc, table, w, x, wx, b, c, offs, out):
         nc.vector.memset(scratch[:], 0.0)
         nc.scalar.activation(scratch[:], scratch[:], SIGMOID)
 
+        zeros = held.tile([P, P], BF16, name="zeros")
+        nc.vector.memset(zeros[:], 0.0)
+        unread = psum.tile([P, P], F32, name="unread")
+        for i in range(WARMING_MATMULS):
+            nc.tensor.matmul(unread[:], zeros[:], zeros[:], start=True, stop=True)
+
         pre = [psum.tile([P, N], F32, name=f"pre{g}") for g in range(GATES)]
         gate_order = (FORGET, IN_GATE, UPDATE, OUT_GATE)
         for g in gate_order:
-            nc.tensor.matmul(pre[g][:], wx_sb[:, g * P : (g + 1) * P], x_sb[:], start=True, stop=False)
-        for g in gate_order:
             nc.tensor.matmul(
-                pre[g][:], w_sb[:, g * P : (g + 1) * P], store[:].indirect(offsets[:]), start=False, stop=True
+                pre[g][:], w_sb[:, g * P : (g + 1) * P], store[:].indirect(offsets[:]), start=True, stop=False
             )
+        for g in gate_order:
+            nc.tensor.matmul(pre[g][:], wx_sb[:, g * P : (g + 1) * P], x_sb[:], start=False, stop=True)
 
         def gate(g, func, name):
             result = held.tile([P, N], F32, name=name)

@@ -32,7 +32,7 @@ def tile_narytreelstmcell_kernel(tc, table, w, x, wx, b, c, offs, out):
         x_sb = held.tile([P, N], BF16, name="x_sb")
         nc.sync.dma_start(x_sb[:], x)
         c_sb = held.tile([P, N], F32, name="c_sb")
-        nc.gpsimd.dma_start(c_sb[:], c)
+        nc.scalar.dma_start(c_sb[:], c)
         bias = held.tile([P, GATES], F32, name="bias")
         with nc.allow_non_contiguous_dma(reason="512 bias values, one to a partition and gate"):
             nc.sync.dma_start(bias[:], b.rearrange("(g r) o -> r (g o)", r=P))

@@ -7,6 +7,7 @@ TANH = mybir.ActivationFunctionType.Tanh
 P = 128
 S = 512
 N = 128
+BLOCK = 8
 GATES = 4
 IN_GATE, OUT_GATE, UPDATE, FORGET = 0, 1, 2, 3
 
@@ -33,9 +34,9 @@ def tile_narytreelstmcell_kernel(tc, table, w, x, wx, b, c, offs, out):
         nc.sync.dma_start(x_sb[:], x)
         c_sb = held.tile([P, N], F32, name="c_sb")
         nc.scalar.dma_start(c_sb[:], c)
-        bias = held.tile([P, GATES], F32, name="bias")
+        bias = held.tile([P, GATES, BLOCK], F32, name="bias")
         with nc.allow_non_contiguous_dma(reason="512 bias values, one to a partition and gate"):
-            nc.sync.dma_start(bias[:], b.rearrange("(g r) o -> r (g o)", r=P))
+            nc.sync.dma_start(bias[:, :, 0:1], b.rearrange("(g r) o -> r g o", r=P))
 
         scratch = held.tile([P, 1], F32, name="scratch")
         nc.vector.memset(scratch[:], 0.0)
@@ -58,7 +59,7 @@ def tile_narytreelstmcell_kernel(tc, table, w, x, wx, b, c, offs, out):
 
         def gate(g, func, name):
             result = held.tile([P, N], F32, name=name)
-            nc.scalar.activation(result[:], pre[g][:], func, bias=bias[:, g : g + 1])
+            nc.scalar.activation(result[:], pre[g][:], func, bias=bias[:, g, 0:1])
             return result
 
         forget = gate(FORGET, SIGMOID, "forget")

@@ -32,11 +32,13 @@ def tile_narytreelstmcell_kernel(tc, table, w, x, wx, b, c, offs, out):
         nc.scalar.dma_start(wx_sb[:], wx)
         x_sb = held.tile([P, N], BF16, name="x_sb")
         nc.sync.dma_start(x_sb[:], x)
-        c_sb = held.tile([P, N], F32, name="c_sb")
-        nc.scalar.dma_start(c_sb[:], c)
         bias = held.tile([P, GATES, BLOCK], F32, name="bias")
+        b_columns = b.rearrange("(g r) o -> r g o", r=P)
         with nc.allow_non_contiguous_dma(reason="512 bias values, one to a partition and gate"):
-            nc.sync.dma_start(bias[:, :, 0:1], b.rearrange("(g r) o -> r g o", r=P))
+            for pair in (slice(UPDATE, FORGET + 1), slice(IN_GATE, OUT_GATE + 1)):
+                nc.sync.dma_start(bias[:, pair, 0:1], b_columns[:, pair, :])
+        c_sb = held.tile([P, N], F32, name="c_sb")
+        nc.sync.dma_start(c_sb[:], c)
 
         scratch = held.tile([P, 1], F32, name="scratch")
         nc.vector.memset(scratch[:], 0.0)
@@ -49,7 +51,7 @@ def tile_narytreelstmcell_kernel(tc, table, w, x, wx, b, c, offs, out):
             nc.tensor.matmul(unread[:], zeros[:], zeros[:], start=True, stop=True)
 
         pre = [psum.tile([P, N], F32, name=f"pre{g}") for g in range(GATES)]
-        gate_order = (FORGET, IN_GATE, UPDATE, OUT_GATE)
+        gate_order = (FORGET, UPDATE, IN_GATE, OUT_GATE)
         for g in gate_order:
             nc.tensor.matmul(
                 pre[g][:], w_sb[:, g * P : (g + 1) * P], store[:].indirect(offsets[:]), start=True, stop=False
@@ -63,8 +65,8 @@ def tile_narytreelstmcell_kernel(tc, table, w, x, wx, b, c, offs, out):
             return result
 
         forget = gate(FORGET, SIGMOID, "forget")
-        in_gate = gate(IN_GATE, SIGMOID, "in_gate")
         update = gate(UPDATE, TANH, "update")
+        in_gate = gate(IN_GATE, SIGMOID, "in_gate")
         out_gate = gate(OUT_GATE, SIGMOID, "out_gate")
 
         kept = held.tile([P, N], F32, name="kept")

@@ -26,19 +26,17 @@ def tile_narytreelstmcell_kernel(tc, table, w, x, wx, b, c, offs, out):
         nc.sync.dma_start(offsets[:], offs)
         store = held.tile([P, S], BF16, name="store")
         nc.sync.dma_start(store[:], table)
+        bias = held.tile([P, GATES, BLOCK], F32, name="bias")
+        with nc.allow_non_contiguous_dma(reason="512 bias values, one to a partition and gate"):
+            nc.scalar.dma_start(bias[:, :, 0:1], b.rearrange("(g r) o -> r g o", r=P))
         w_sb = held.tile([P, GATES * P], BF16, name="w_sb")
         nc.scalar.dma_start(w_sb[:], w)
         wx_sb = held.tile([P, GATES * P], BF16, name="wx_sb")
         nc.scalar.dma_start(wx_sb[:], wx)
         x_sb = held.tile([P, N], BF16, name="x_sb")
         nc.sync.dma_start(x_sb[:], x)
-        bias = held.tile([P, GATES, BLOCK], F32, name="bias")
-        b_columns = b.rearrange("(g r) o -> r g o", r=P)
-        with nc.allow_non_contiguous_dma(reason="512 bias values, one to a partition and gate"):
-            for pair in (slice(UPDATE, FORGET + 1), slice(IN_GATE, OUT_GATE + 1)):
-                nc.sync.dma_start(bias[:, pair, 0:1], b_columns[:, pair, :])
         c_sb = held.tile([P, N], F32, name="c_sb")
-        nc.sync.dma_start(c_sb[:], c)
+        nc.gpsimd.dma_start(c_sb[:], c)
 
         scratch = held.tile([P, 1], F32, name="scratch")
         nc.vector.memset(scratch[:], 0.0)
@@ -51,7 +49,7 @@ def tile_narytreelstmcell_kernel(tc, table, w, x, wx, b, c, offs, out):
             nc.tensor.matmul(unread[:], zeros[:], zeros[:], start=True, stop=True)
 
         pre = [psum.tile([P, N], F32, name=f"pre{g}") for g in range(GATES)]
-        gate_order = (FORGET, UPDATE, IN_GATE, OUT_GATE)
+        gate_order = (FORGET, IN_GATE, UPDATE, OUT_GATE)
         for g in gate_order:
             nc.tensor.matmul(
                 pre[g][:], w_sb[:, g * P : (g + 1) * P], store[:].indirect(offsets[:]), start=True, stop=False
@@ -65,8 +63,8 @@ def tile_narytreelstmcell_kernel(tc, table, w, x, wx, b, c, offs, out):
             return result
 
         forget = gate(FORGET, SIGMOID, "forget")
-        update = gate(UPDATE, TANH, "update")
         in_gate = gate(IN_GATE, SIGMOID, "in_gate")
+        update = gate(UPDATE, TANH, "update")
         out_gate = gate(OUT_GATE, SIGMOID, "out_gate")
 
         kept = held.tile([P, N], F32, name="kept")

@@ -11,7 +11,7 @@ BLOCK = 8
 GATES = 4
 IN_GATE, OUT_GATE, UPDATE, FORGET = 0, 1, 2, 3
 
-WARMING_MATMULS = 16
+WARMING_MATMULS = 12
 
 FLOPS = 2 * (P + P) * (GATES * P) * N
 
@@ -22,21 +22,21 @@ def tile_narytreelstmcell_kernel(tc, table, w, x, wx, b, c, offs, out):
         tc.tile_pool(name="held", bufs=1) as held,
         tc.psum_pool(name="psum", bufs=1) as psum,
     ):
-        offsets = held.tile([P, N // 16], U16, name="offsets")
-        nc.sync.dma_start(offsets[:], offs)
-        store = held.tile([P, S], BF16, name="store")
-        nc.sync.dma_start(store[:], table)
-        bias = held.tile([P, GATES, BLOCK], F32, name="bias")
-        with nc.allow_non_contiguous_dma(reason="512 bias values, one to a partition and gate"):
-            nc.scalar.dma_start(bias[:, :, 0:1], b.rearrange("(g r) o -> r g o", r=P))
-        w_sb = held.tile([P, GATES * P], BF16, name="w_sb")
-        nc.scalar.dma_start(w_sb[:], w)
-        wx_sb = held.tile([P, GATES * P], BF16, name="wx_sb")
-        nc.scalar.dma_start(wx_sb[:], wx)
         x_sb = held.tile([P, N], BF16, name="x_sb")
         nc.sync.dma_start(x_sb[:], x)
+        wx_sb = held.tile([P, GATES * P], BF16, name="wx_sb")
+        nc.scalar.dma_start(wx_sb[:], wx)
+        store = held.tile([P, S], BF16, name="store")
+        nc.sync.dma_start(store[:], table)
+        w_sb = held.tile([P, GATES * P], BF16, name="w_sb")
+        nc.scalar.dma_start(w_sb[:], w)
+        offsets = held.tile([P, N // 16], U16, name="offsets")
+        nc.sync.dma_start(offsets[:], offs)
         c_sb = held.tile([P, N], F32, name="c_sb")
-        nc.gpsimd.dma_start(c_sb[:], c)
+        nc.scalar.dma_start(c_sb[:], c)
+        bias = held.tile([P, GATES, BLOCK], F32, name="bias")
+        with nc.allow_non_contiguous_dma(reason="512 bias values, one to a partition and gate"):
+            nc.sync.dma_start(bias[:, :, 0:1], b.rearrange("(g r) o -> r g o", r=P))
 
         scratch = held.tile([P, 1], F32, name="scratch")
         nc.vector.memset(scratch[:], 0.0)
@@ -51,11 +51,11 @@ def tile_narytreelstmcell_kernel(tc, table, w, x, wx, b, c, offs, out):
         pre = [psum.tile([P, N], F32, name=f"pre{g}") for g in range(GATES)]
         gate_order = (FORGET, IN_GATE, UPDATE, OUT_GATE)
         for g in gate_order:
-            nc.tensor.matmul(
-                pre[g][:], w_sb[:, g * P : (g + 1) * P], store[:].indirect(offsets[:]), start=True, stop=False
-            )
+            nc.tensor.matmul(pre[g][:], wx_sb[:, g * P : (g + 1) * P], x_sb[:], start=True, stop=False)
         for g in gate_order:
-            nc.tensor.matmul(pre[g][:], wx_sb[:, g * P : (g + 1) * P], x_sb[:], start=False, stop=True)
+            nc.tensor.matmul(
+                pre[g][:], w_sb[:, g * P : (g + 1) * P], store[:].indirect(offsets[:]), start=False, stop=True
+            )
 
         def gate(g, func, name):
             result = held.tile([P, N], F32, name=name)

@@ -8,6 +8,7 @@ P = 128
 S = 512
 N = 128
 BLOCK = 8
+HALF = N // 2
 GATES = 4
 IN_GATE, OUT_GATE, UPDATE, FORGET = 0, 1, 2, 3
 
@@ -57,23 +58,29 @@ def tile_narytreelstmcell_kernel(tc, table, w, x, wx, b, c, offs, out):
                 pre[g][:], w_sb[:, g * P : (g + 1) * P], store[:].indirect(offsets[:]), start=False, stop=True
             )
 
-        def gate(g, func, name):
-            result = held.tile([P, N], F32, name=name)
-            nc.scalar.activation(result[:], pre[g][:], func, bias=bias[:, g, 0:1])
+        def gate(g, func, name, first=0, width=N):
+            result = held.tile([P, width], F32, name=name)
+            nc.scalar.activation(result[:], pre[g][:, first : first + width], func, bias=bias[:, g, 0:1])
             return result
 
+        halves = (0, 1)
         forget = gate(FORGET, SIGMOID, "forget")
         in_gate = gate(IN_GATE, SIGMOID, "in_gate")
-        update = gate(UPDATE, TANH, "update")
+        update = [gate(UPDATE, TANH, f"update{h}", h * HALF, HALF) for h in halves]
         out_gate = gate(OUT_GATE, SIGMOID, "out_gate")
 
         kept = held.tile([P, N], F32, name="kept")
         nc.vector.tensor_mul(kept[:], forget[:], c_sb[:])
-        c_new = held.tile([P, N], F32, name="c_new")
-        nc.vector.tensor_mul(c_new[:], in_gate[:], update[:])
-        nc.vector.tensor_add(c_new[:], c_new[:], kept[:])
-        squashed = held.tile([P, N], F32, name="squashed")
-        nc.scalar.activation(squashed[:], c_new[:], TANH)
-        hidden = held.tile([P, N], F32, name="hidden")
-        nc.vector.tensor_mul(hidden[:], out_gate[:], squashed[:])
-        nc.sync.dma_start(out, hidden[:])
+        added = [held.tile([P, HALF], F32, name=f"added{h}") for h in halves]
+        c_new = [held.tile([P, HALF], F32, name=f"c_new{h}") for h in halves]
+        squashed = [held.tile([P, HALF], F32, name=f"squashed{h}") for h in halves]
+        hidden = [held.tile([P, HALF], F32, name=f"hidden{h}") for h in halves]
+        for h in halves:
+            nc.vector.tensor_mul(added[h][:], in_gate[:, h * HALF : (h + 1) * HALF], update[h][:])
+        for h in halves:
+            nc.vector.tensor_add(c_new[h][:], added[h][:], kept[:, h * HALF : (h + 1) * HALF])
+        for h in halves:
+            nc.scalar.activation(squashed[h][:], c_new[h][:], TANH)
+        for h in halves:
+            nc.vector.tensor_mul(hidden[h][:], out_gate[:, h * HALF : (h + 1) * HALF], squashed[h][:])
+            nc.sync.dma_start(out[:, h * HALF : (h + 1) * HALF], hidden[h][:])

@@ -74,7 +74,7 @@ def tile_narytreelstmcell_kernel(tc, table, w, x, wx, b, c, offs, out):
         added = [held.tile([P, HALF], F32, name=f"added{h}") for h in halves]
         c_new = [held.tile([P, HALF], F32, name=f"c_new{h}") for h in halves]
         squashed = [held.tile([P, HALF], F32, name=f"squashed{h}") for h in halves]
-        hidden = [held.tile([P, HALF], F32, name=f"hidden{h}") for h in halves]
+        hidden = held.tile([P, N], F32, name="hidden")
         for h in halves:
             nc.vector.tensor_mul(added[h][:], in_gate[:, h * HALF : (h + 1) * HALF], update[h][:])
         for h in halves:
@@ -82,5 +82,7 @@ def tile_narytreelstmcell_kernel(tc, table, w, x, wx, b, c, offs, out):
         for h in halves:
             nc.scalar.activation(squashed[h][:], c_new[h][:], TANH)
         for h in halves:
-            nc.vector.tensor_mul(hidden[h][:], out_gate[:, h * HALF : (h + 1) * HALF], squashed[h][:])
-            nc.sync.dma_start(out[:, h * HALF : (h + 1) * HALF], hidden[h][:])
+            nc.vector.tensor_mul(
+                hidden[:, h * HALF : (h + 1) * HALF], out_gate[:, h * HALF : (h + 1) * HALF], squashed[h][:]
+            )
+        nc.sync.dma_start(out, hidden[:])

@@ -8,7 +8,8 @@ P = 128
 S = 512
 N = 128
 BLOCK = 8
-HALF = N // 2
+PIECES = 4
+WIDTH = N // PIECES
 GATES = 4
 IN_GATE, OUT_GATE, UPDATE, FORGET = 0, 1, 2, 3
 
@@ -63,26 +64,26 @@ def tile_narytreelstmcell_kernel(tc, table, w, x, wx, b, c, offs, out):
             nc.scalar.activation(result[:], pre[g][:, first : first + width], func, bias=bias[:, g, 0:1])
             return result
 
-        halves = (0, 1)
+        pieces = range(PIECES)
         forget = gate(FORGET, SIGMOID, "forget")
         in_gate = gate(IN_GATE, SIGMOID, "in_gate")
-        update = [gate(UPDATE, TANH, f"update{h}", h * HALF, HALF) for h in halves]
+        update = [gate(UPDATE, TANH, f"update{i}", i * WIDTH, WIDTH) for i in pieces]
         out_gate = gate(OUT_GATE, SIGMOID, "out_gate")
 
         kept = held.tile([P, N], F32, name="kept")
         nc.vector.tensor_mul(kept[:], forget[:], c_sb[:])
-        added = [held.tile([P, HALF], F32, name=f"added{h}") for h in halves]
-        c_new = [held.tile([P, HALF], F32, name=f"c_new{h}") for h in halves]
-        squashed = [held.tile([P, HALF], F32, name=f"squashed{h}") for h in halves]
+        added = [held.tile([P, WIDTH], F32, name=f"added{i}") for i in pieces]
+        c_new = [held.tile([P, WIDTH], F32, name=f"c_new{i}") for i in pieces]
+        squashed = [held.tile([P, WIDTH], F32, name=f"squashed{i}") for i in pieces]
         hidden = held.tile([P, N], F32, name="hidden")
-        for h in halves:
-            nc.vector.tensor_mul(added[h][:], in_gate[:, h * HALF : (h + 1) * HALF], update[h][:])
-        for h in halves:
-            nc.vector.tensor_add(c_new[h][:], added[h][:], kept[:, h * HALF : (h + 1) * HALF])
-        for h in halves:
-            nc.scalar.activation(squashed[h][:], c_new[h][:], TANH)
-        for h in halves:
+        for i in pieces:
+            nc.vector.tensor_mul(added[i][:], in_gate[:, i * WIDTH : (i + 1) * WIDTH], update[i][:])
+        for i in pieces:
+            nc.vector.tensor_add(c_new[i][:], added[i][:], kept[:, i * WIDTH : (i + 1) * WIDTH])
+        for i in pieces:
+            nc.scalar.activation(squashed[i][:], c_new[i][:], TANH)
+        for i in pieces:
             nc.vector.tensor_mul(
-                hidden[:, h * HALF : (h + 1) * HALF], out_gate[:, h * HALF : (h + 1) * HALF], squashed[h][:]
+                hidden[:, i * WIDTH : (i + 1) * WIDTH], out_gate[:, i * WIDTH : (i + 1) * WIDTH], squashed[i][:]
             )
         nc.sync.dma_start(out, hidden[:])

@@ -27,18 +27,18 @@ def tile_narytreelstmcell_kernel(tc, table, w, x, wx, b, c, offs, out):
         x_sb = held.tile([P, N], BF16, name="x_sb")
         nc.sync.dma_start(x_sb[:], x)
         wx_sb = held.tile([P, GATES * P], BF16, name="wx_sb")
-        nc.scalar.dma_start(wx_sb[:], wx)
+        nc.sync.dma_start(wx_sb[:], wx)
+        offsets = held.tile([P, N // 16], U16, name="offsets")
+        nc.sync.dma_start(offsets[:], offs)
         store = held.tile([P, S], BF16, name="store")
         nc.sync.dma_start(store[:], table)
         w_sb = held.tile([P, GATES * P], BF16, name="w_sb")
-        nc.scalar.dma_start(w_sb[:], w)
-        offsets = held.tile([P, N // 16], U16, name="offsets")
-        nc.sync.dma_start(offsets[:], offs)
-        c_sb = held.tile([P, N], F32, name="c_sb")
-        nc.scalar.dma_start(c_sb[:], c)
+        nc.sync.dma_start(w_sb[:], w)
         bias = held.tile([P, GATES, BLOCK], F32, name="bias")
         with nc.allow_non_contiguous_dma(reason="512 bias values, one to a partition and gate"):
             nc.sync.dma_start(bias[:, :, 0:1], b.rearrange("(g r) o -> r g o", r=P))
+        c_sb = held.tile([P, N], F32, name="c_sb")
+        nc.sync.dma_start(c_sb[:], c)
 
         scratch = held.tile([P, 1], F32, name="scratch")
         nc.vector.memset(scratch[:], 0.0)

@@ -51,13 +51,20 @@ def tile_narytreelstmcell_kernel(tc, table, w, x, wx, b, c, offs, out):
             nc.tensor.matmul(unread[:], zeros[:], zeros[:], start=True, stop=True)
 
         pre = [psum.tile([P, N], F32, name=f"pre{g}") for g in range(GATES)]
-        gate_order = (FORGET, IN_GATE, UPDATE, OUT_GATE)
-        for g in gate_order:
-            nc.tensor.matmul(pre[g][:], wx_sb[:, g * P : (g + 1) * P], x_sb[:], start=True, stop=False)
-        for g in gate_order:
-            nc.tensor.matmul(
-                pre[g][:], w_sb[:, g * P : (g + 1) * P], store[:].indirect(offsets[:]), start=False, stop=True
-            )
+
+        def x_part(g, first):
+            nc.tensor.matmul(pre[g][:], wx_sb[:, g * P : (g + 1) * P], x_sb[:], start=first, stop=not first)
+
+        def gathered_part(g, first):
+            looked_up = store[:].indirect(offsets[:])
+            nc.tensor.matmul(pre[g][:], w_sb[:, g * P : (g + 1) * P], looked_up, start=first, stop=not first)
+
+        for g in (FORGET, IN_GATE, UPDATE):
+            x_part(g, first=True)
+        for g in (FORGET, IN_GATE, UPDATE):
+            gathered_part(g, first=False)
+        gathered_part(OUT_GATE, first=True)
+        x_part(OUT_GATE, first=False)
 
         def gate(g, func, name, first=0, width=N):
             result = held.tile([P, width], F32, name=name)

@@ -13,8 +13,6 @@ WIDTH = N // PIECES
 GATES = 4
 IN_GATE, OUT_GATE, UPDATE, FORGET = 0, 1, 2, 3
 
-WARMING_MATMULS = 12
-
 FLOPS = 2 * (P + P) * (GATES * P) * N
 
 
@@ -43,12 +41,6 @@ def tile_narytreelstmcell_kernel(tc, table, w, x, wx, b, c, offs, out):
         scratch = held.tile([P, 1], F32, name="scratch")
         nc.vector.memset(scratch[:], 0.0)
         nc.scalar.activation(scratch[:], scratch[:], SIGMOID)
-
-        zeros = held.tile([P, P], BF16, name="zeros")
-        nc.vector.memset(zeros[:], 0.0)
-        unread = psum.tile([P, P], F32, name="unread")
-        for i in range(WARMING_MATMULS):
-            nc.tensor.matmul(unread[:], zeros[:], zeros[:], start=True, stop=True)
 
         pre = [psum.tile([P, N], F32, name=f"pre{g}") for g in range(GATES)]
 

@@ -30,8 +30,10 @@ def tile_narytreelstmcell_kernel(tc, table, w, x, wx, b, c, offs, out):
         nc.sync.dma_start(offsets[:], offs)
         store = held.tile([P, S], BF16, name="store")
         nc.sync.dma_start(store[:], table)
-        w_sb = held.tile([P, GATES * P], BF16, name="w_sb")
-        nc.sync.dma_start(w_sb[:], w)
+        w_forget = held.tile([P, P], BF16, name="w_forget")
+        nc.sync.dma_start(w_forget[:], w[:, FORGET * P : (FORGET + 1) * P])
+        w_others = held.tile([P, FORGET * P], BF16, name="w_others")
+        nc.sync.dma_start(w_others[:], w[:, 0 : FORGET * P])
         bias = held.tile([P, GATES, BLOCK], F32, name="bias")
         with nc.allow_non_contiguous_dma(reason="512 bias values, one to a partition and gate"):
             nc.sync.dma_start(bias[:, :, 0:1], b.rearrange("(g r) o -> r g o", r=P))
@@ -49,7 +51,8 @@ def tile_narytreelstmcell_kernel(tc, table, w, x, wx, b, c, offs, out):
 
         def gathered_part(g, first):
             looked_up = store[:].indirect(offsets[:])
-            nc.tensor.matmul(pre[g][:], w_sb[:, g * P : (g + 1) * P], looked_up, start=first, stop=not first)
+            w_block = w_forget[:] if g == FORGET else w_others[:, g * P : (g + 1) * P]
+            nc.tensor.matmul(pre[g][:], w_block, looked_up, start=first, stop=not first)
 
         for g in (FORGET, IN_GATE, UPDATE):
             x_part(g, first=True)

@@ -38,7 +38,7 @@ def tile_narytreelstmcell_kernel(tc, table, w, x, wx, b, c, offs, out):
         with nc.allow_non_contiguous_dma(reason="512 bias values, one to a partition and gate"):
             nc.sync.dma_start(bias[:, :, 0:1], b.rearrange("(g r) o -> r g o", r=P))
         c_sb = held.tile([P, N], F32, name="c_sb")
-        nc.sync.dma_start(c_sb[:], c)
+        nc.gpsimd.dma_start(c_sb[:], c)
 
         scratch = held.tile([P, 1], F32, name="scratch")
         nc.vector.memset(scratch[:], 0.0)

@@ -12,6 +12,7 @@ PIECES = 4
 WIDTH = N // PIECES
 GATES = 4
 IN_GATE, OUT_GATE, UPDATE, FORGET = 0, 1, 2, 3
+HOLD_COLUMNS = 2 * P
 
 FLOPS = 2 * (P + P) * (GATES * P) * N
 
@@ -37,6 +38,8 @@ def tile_narytreelstmcell_kernel(tc, table, w, x, wx, b, c, offs, out):
         bias = held.tile([P, GATES, BLOCK], F32, name="bias")
         with nc.allow_non_contiguous_dma(reason="512 bias values, one to a partition and gate"):
             nc.sync.dma_start(bias[:, :, 0:1], b.rearrange("(g r) o -> r g o", r=P))
+        held_back = held.tile([P, HOLD_COLUMNS], F32, name="held_back")
+        nc.gpsimd.memset(held_back[:], 0.0)
         c_sb = held.tile([P, N], F32, name="c_sb")
         nc.gpsimd.dma_start(c_sb[:], c)
 

import concourse.mybir as mybir

BF16, F32, U16 = mybir.dt.bfloat16, mybir.dt.float32, mybir.dt.uint16
SIGMOID = mybir.ActivationFunctionType.Sigmoid
TANH = mybir.ActivationFunctionType.Tanh

P = 128
S = 512
N = 128
BLOCK = 8
PIECES = 4
WIDTH = N // PIECES
GATES = 4
IN_GATE, OUT_GATE, UPDATE, FORGET = 0, 1, 2, 3
HOLD_COLUMNS = 2 * P

FLOPS = 2 * (P + P) * (GATES * P) * N


def tile_narytreelstmcell_kernel(tc, table, w, x, wx, b, c, offs, out):
    nc = tc.nc
    with (
        tc.tile_pool(name="held", bufs=1) as held,
        tc.psum_pool(name="psum", bufs=1) as psum,
    ):
        x_sb = held.tile([P, N], BF16, name="x_sb")
        nc.sync.dma_start(x_sb[:], x)
        wx_sb = held.tile([P, GATES * P], BF16, name="wx_sb")
        nc.sync.dma_start(wx_sb[:], wx)
        offsets = held.tile([P, N // 16], U16, name="offsets")
        nc.sync.dma_start(offsets[:], offs)
        store = held.tile([P, S], BF16, name="store")
        nc.sync.dma_start(store[:], table)
        w_forget = held.tile([P, P], BF16, name="w_forget")
        nc.sync.dma_start(w_forget[:], w[:, FORGET * P : (FORGET + 1) * P])
        w_others = held.tile([P, FORGET * P], BF16, name="w_others")
        nc.sync.dma_start(w_others[:], w[:, 0 : FORGET * P])
        bias = held.tile([P, GATES, BLOCK], F32, name="bias")
        with nc.allow_non_contiguous_dma(reason="512 bias values, one to a partition and gate"):
            nc.sync.dma_start(bias[:, :, 0:1], b.rearrange("(g r) o -> r g o", r=P))
        held_back = held.tile([P, HOLD_COLUMNS], F32, name="held_back")
        nc.gpsimd.memset(held_back[:], 0.0)
        c_sb = held.tile([P, N], F32, name="c_sb")
        nc.gpsimd.dma_start(c_sb[:], c)

        scratch = held.tile([P, 1], F32, name="scratch")
        nc.vector.memset(scratch[:], 0.0)
        nc.scalar.activation(scratch[:], scratch[:], SIGMOID)

        pre = [psum.tile([P, N], F32, name=f"pre{g}") for g in range(GATES)]

        def x_part(g, first):
            nc.tensor.matmul(pre[g][:], wx_sb[:, g * P : (g + 1) * P], x_sb[:], start=first, stop=not first)

        def gathered_part(g, first):
            looked_up = store[:].indirect(offsets[:])
            w_block = w_forget[:] if g == FORGET else w_others[:, g * P : (g + 1) * P]
            nc.tensor.matmul(pre[g][:], w_block, looked_up, start=first, stop=not first)

        for g in (FORGET, IN_GATE, UPDATE):
            x_part(g, first=True)
        for g in (FORGET, IN_GATE, UPDATE):
            gathered_part(g, first=False)
        gathered_part(OUT_GATE, first=True)
        x_part(OUT_GATE, first=False)

        def gate(g, func, name, first=0, width=N):
            result = held.tile([P, width], F32, name=name)
            nc.scalar.activation(result[:], pre[g][:, first : first + width], func, bias=bias[:, g, 0:1])
            return result

        pieces = range(PIECES)
        forget = gate(FORGET, SIGMOID, "forget")
        in_gate = gate(IN_GATE, SIGMOID, "in_gate")
        update = [gate(UPDATE, TANH, f"update{i}", i * WIDTH, WIDTH) for i in pieces]
        out_gate = gate(OUT_GATE, SIGMOID, "out_gate")

        kept = held.tile([P, N], F32, name="kept")
        nc.vector.tensor_mul(kept[:], forget[:], c_sb[:])
        added = [held.tile([P, WIDTH], F32, name=f"added{i}") for i in pieces]
        c_new = [held.tile([P, WIDTH], F32, name=f"c_new{i}") for i in pieces]
        squashed = [held.tile([P, WIDTH], F32, name=f"squashed{i}") for i in pieces]
        hidden = held.tile([P, N], F32, name="hidden")
        for i in pieces:
            nc.vector.tensor_mul(added[i][:], in_gate[:, i * WIDTH : (i + 1) * WIDTH], update[i][:])
        for i in pieces:
            nc.vector.tensor_add(c_new[i][:], added[i][:], kept[:, i * WIDTH : (i + 1) * WIDTH])
        for i in pieces:
            nc.scalar.activation(squashed[i][:], c_new[i][:], TANH)
        for i in pieces:
            nc.vector.tensor_mul(
                hidden[:, i * WIDTH : (i + 1) * WIDTH], out_gate[:, i * WIDTH : (i + 1) * WIDTH], squashed[i][:]
            )
        nc.sync.dma_start(out, hidden[:])
